import numpy as np
import ml_dtypes


def mxq(x, axis, fmt="e4m3"):
    dtype, down = {"e4m3": (ml_dtypes.float8_e4m3fn, 7), "e5m2": (ml_dtypes.float8_e5m2, 14)}[fmt]
    v = np.moveaxis(np.asarray(x, np.float32).astype(ml_dtypes.bfloat16).astype(np.float64), axis, -1)
    blocks = v.reshape(v.shape[:-1] + (-1, 32))
    amax = np.abs(blocks).max(-1, keepdims=True)
    byte = np.maximum(np.where(amax > 0, np.frexp(amax)[1] - 1 + 127, 0) - down, 1)
    scale = np.exp2(byte - 127.0)
    codes = (blocks / scale).astype(np.float32).astype(dtype).astype(np.float64)
    return np.moveaxis((codes * scale).reshape(v.shape), -1, axis)


WIDE = False


def mx_kscale(k):
    if not WIDE:
        return np.ones(k)
    levels = np.array([10, -10, 5, -5, 0])
    if k % 512:
        return np.exp2(np.random.permutation(np.resize(levels, k // 32))).repeat(32)
    a = np.empty((k // 512, 16))
    for p in range(k // 512):
        a[p, :8] = np.random.permutation(np.resize(levels, 8))
        for g in range(8):
            far = levels[np.abs(levels - a[p, g]) >= 10]
            a[p, g + 8] = far[np.random.randint(len(far))]
    return np.exp2(a.ravel()).repeat(32)


BF16 = ml_dtypes.bfloat16


def bf(x):
    return np.asarray(x, np.float32).astype(BF16)


def f64(x):
    return np.asarray(x).astype(np.float64)


B, H, N, NMAX, NMIN, V, VI, NH = 4096, 512, 127, 127, 126, 16, 3, 2
TS = 4.0


def distortion(X):
    cols = [np.sum(X[:, :-k] * X[:, k:], axis=1) for k in range(1, N + 1)]
    return np.stack(cols[::-1], axis=1)


def setup_inputs():
    s, t = mx_kscale(H), mx_kscale(H)
    return {"h1": bf(np.maximum(np.random.standard_normal((B, H)), 0.0) * s),
            "w_hid2": bf(np.random.standard_normal((H, H)) * 1.5 / np.sqrt(H) * t[:, None] / s[None, :]),
            "b_hid2": bf(np.random.standard_normal(H) * 0.2 * t),
            "w_out": bf(np.random.standard_normal((N + 1, H)) * 0.18 / np.sqrt(H) / t[None, :]),
            "b_out": bf(np.random.standard_normal(N + 1) * 0.03),
            "norm_root": bf(np.sqrt(TS * np.sqrt(N)) * np.exp(0.15 * np.random.standard_normal((B, 1)))),
            "T": bf(np.random.standard_normal((B, N)) * TS)}


def reference(h1, w_hid2, b_hid2, w_out, b_out, norm_root, T):
    h2 = np.maximum((mxq(f64(h1), 1, "e4m3") @ mxq(f64(w_hid2), 1, "e4m3").T) + f64(b_hid2), 0.0)
    X_hat = ((mxq(h2, 1, "e4m3") @ mxq(f64(w_out), 1, "e4m3").T) + f64(b_out)) * f64(norm_root)
    X_hat_clamped = np.clip(X_hat, -2.0, 2.0)
    error = np.reshape(np.mean((distortion(X_hat) - f64(T)) ** 2), (1,))
    error_clamped = np.reshape(np.mean((distortion(X_hat_clamped) - f64(T)) ** 2), (1,))
    return (X_hat, error, X_hat_clamped, error_clamped)

@@ -1,0 +1,413 @@
+from contextlib import ExitStack
+import math
+
+import concourse.mybir as mybir
+from concourse.masks import make_identity
+
+F32 = mybir.dt.float32
+BF16 = mybir.dt.bfloat16
+I32 = mybir.dt.int32
+U32 = mybir.dt.uint32
+U8 = mybir.dt.uint8
+FP8X4 = mybir.dt.float8_e4m3fn_x4
+ALU = mybir.AluOpType
+ACT = mybir.ActivationFunctionType
+AX = mybir.AxisListType
+
+BANK_DT = F32
+
+P = 128
+ROWS, HID, NOUT, NLAG = 4096, 512, 128, 127
+NT = ROWS // P
+TPC = 4
+NCH = NT // TPC
+NVCH = 5
+TAIL0 = 2 * TPC * NVCH
+LANES = TAIL0 + TPC * (NCH - NVCH)
+NSTAGE = 7
+NEARLY = 4
+NPIECE = 8
+V_INTERLEAVES = (0, 1)
+FP = NOUT // NPIECE
+
+FLOPS = 2 * ROWS * HID * HID + 2 * ROWS * HID * NOUT
+
+
+def tree_levels():
+    levels = [[-math.pi / 2]]
+    for s in range(NSTAGE):
+        levels.append([w for v in levels[s] for w in (v / 2, v / 2 + math.pi)])
+    return levels
+
+
+def tile_qdtssolveronnx_pa_kernel(tc, h1, w_hid2, b_hid2, w_out, b_out, norm_root, T, out_0, out_1, out_2, out_3):
+    nc = tc.nc
+    h1v = h1.rearrange("(p t) k -> p t k", t=NT)
+    x_out = out_0.rearrange("(p t) n -> p t n", t=NT)
+    xc_out = out_2.rearrange("(p t) n -> p t n", t=NT)
+    levels = tree_levels()
+
+    def stt(out, in0, scalar, in1, op1=ALU.add):
+        nc.vector.scalar_tensor_tensor(out=out, in0=in0, scalar=scalar, in1=in1, op0=ALU.mult, op1=op1)
+
+    def stage(s, sr, si, dr, di, merged, nodes):
+        size = NOUT >> s
+        h = size // 2
+        rs = [(math.cos(v / 2), math.sin(v / 2)) for v in levels[s]]
+        for which in range(4):
+            for i in nodes:
+                rr, ri = rs[i]
+                top, bot = slice(i * size, i * size + h), slice(i * size + h, (i + 1) * size)
+                if which == 0:
+                    stt(dr[:, top, :], sr[:, bot, :], rr, sr[:, top, :])
+                elif which == 1:
+                    stt(di[:, top, :], si[:, bot, :], rr, si[:, top, :])
+                elif which == 2:
+                    stt(dr[:, top, :], si[:, bot, :], -ri, dr[:, top, :])
+                else:
+                    stt(di[:, top, :], sr[:, bot, :], ri, di[:, top, :])
+        for a, d in ((sr, dr), (si, di)):
+            if merged:
+                rows = slice(nodes[0] * size, (nodes[-1] + 1) * size)
+                av = a[:, rows, :].rearrange("p (i c j) l -> p i c (j l)", c=2, j=h)
+                dv = d[:, rows, :].rearrange("p (i c j) l -> p i c (j l)", c=2, j=h)
+                stt(dv[:, :, 1, :], av[:, :, 0, :], 2.0, dv[:, :, 0, :], ALU.subtract)
+            else:
+                for i in nodes:
+                    top, bot = slice(i * size, i * size + h), slice(i * size + h, (i + 1) * size)
+                    stt(d[:, bot, :], a[:, top, :], 2.0, d[:, top, :], ALU.subtract)
+
+    with ExitStack() as ctx:
+        assert NCH * TPC == NT
+        keep = ctx.enter_context(tc.tile_pool(name="keep", bufs=1))
+
+        ident_f = keep.tile([P, P], F32, name="ident_f")
+        make_identity(nc, ident_f[:])
+        ident_b = keep.tile([P, P], BF16, name="ident_b")
+        make_identity(nc, ident_b[:])
+        ones = keep.tile([P, P], F32, name="ones")
+        tpad = keep.tile([P, NT, P], BF16, name="tpad")
+
+        cs = keep.tile([P, 2 * NOUT], F32, name="cs")
+        w1c = keep.tile([P, HID], U32, name="w1c", align_bytes=64)
+        w1s = keep.tile([P, HID], U8, name="w1s", align_bytes=64)
+        w2c = keep.tile([P, NOUT], U32, name="w2c", align_bytes=64)
+        w2s = keep.tile([P, NOUT], U8, name="w2s", align_bytes=64)
+        b1f = keep.tile([P, 4], F32, name="b1f")
+        nrf = keep.tile([P, NT], F32, name="nrf")
+        bnr = keep.tile([P, NT, NOUT], F32, name="bnr")
+        xT = keep.tile([P, NT - TPC * NVCH, P], F32, name="xT")
+        th2 = keep.tile([P, NOUT, NT], F32, name="th2")
+        r0 = keep.tile([P, 2 * NT], F32, name="r0")
+        acc = keep.tile([P, 2, 2 * NPIECE], F32, name="acc")
+        nc.vector.memset(acc[:], 0.0)
+        gb_re = keep.tile([P, NOUT, LANES], F32, name="gb_re")
+        gb_im = keep.tile([P, NOUT, LANES], F32, name="gb_im")
+
+        def words_t(ps, src):
+            words = src.bitcast(F32)
+            for u in range(2):
+                nc.tensor.transpose(ps[:, u, :], words[:, u : HID // 2 : 2], ident_f[:])
+
+        with ExitStack() as actx:
+            ps_tr = actx.enter_context(tc.psum_pool(name="ps_tr", bufs=2))
+            ps_s1 = actx.enter_context(tc.psum_pool(name="ps_s1", bufs=4))
+            ps_s2 = actx.enter_context(tc.psum_pool(name="ps_s2", bufs=1))
+            ps_tt = actx.enter_context(tc.psum_pool(name="ps_tt", bufs=1))
+            hp = actx.enter_context(tc.tile_pool(name="hp", bufs=3))
+            h1c = {}
+
+            def load(c):
+                h1c[c] = hp.tile([P, TPC, HID], BF16, name="h1c", tag="h1c")
+                nc.sync.dma_start(out=h1c[c][:], in_=h1v[:, c * TPC : (c + 1) * TPC, :])
+
+            with tc.tile_pool(name="prep", bufs=1) as pre:
+                w1raw = pre.tile([P, 4, HID], BF16, name="w1raw")
+                nc.sync.dma_start(out=w1raw[:], in_=w_hid2.rearrange("(m t) k -> m t k", t=4))
+                load(0)
+                w2raw = pre.tile([P, HID], BF16, name="w2raw")
+                nc.sync.dma_start(out=w2raw[:], in_=w_out)
+                b1raw = pre.tile([P, 4], BF16, name="b1raw")
+                nc.sync.dma_start(out=b1raw[:], in_=b_hid2.rearrange("(p t) -> p t", t=4))
+                nrraw = pre.tile([P, NT], BF16, name="nrraw")
+                nc.sync.dma_start(out=nrraw[:], in_=norm_root.rearrange("(p t) o -> p (t o)", t=NT))
+                boraw = pre.tile([P, NOUT], BF16, name="boraw")
+                nc.sync.dma_start(out=boraw[:], in_=b_out.partition_broadcast(P))
+                load(1)
+                load(2)
+
+                nc.vector.tensor_copy(out=b1f[:], in_=b1raw[:])
+                nc.vector.tensor_copy(out=nrf[:], in_=nrraw[:])
+                for tau in range(NT):
+                    nc.gpsimd.tensor_scalar(out=bnr[:, tau, :], in0=boraw[:], scalar1=nrf[:, tau : tau + 1], scalar2=0.0, op0=ALU.mult, op1=ALU.add)
+
+                gw1 = pre.tile([P, 4 * HID], BF16, name="gw1", align_bytes=64)
+                gw1w = gw1[:].bitcast(F32).rearrange("q (t m u) -> q t m u", t=4, u=2)
+                for half in range(2):
+                    ps = ps_tr.tile([P, 2, 2, P], F32, name="ps_w1", tag="tr")
+                    for i in range(2):
+                        words_t(ps[:, i], w1raw[:, 2 * half + i, :])
+                    if half == 0:
+                        nc.vector.tensor_copy(out=gw1w[:, 0:2], in_=ps[:].rearrange("q t u m -> q t m u"))
+                    else:
+                        nc.scalar.copy(out=gw1w[:, 2:4], in_=ps[:].rearrange("q t u m -> q t m u"))
+                nc.vector.quantize_mx(out=w1c[:].bitcast(FP8X4), scales=w1s[:], in_=gw1[:])
+
+                gw2 = pre.tile([P, 4 * NOUT], BF16, name="gw2", align_bytes=64)
+                ps = ps_tr.tile([P, 2, 2, P], F32, name="ps_w2", tag="tr")
+                words_t(ps[:, 0], w2raw[:])
+                nc.vector.tensor_copy(out=gw2[:].bitcast(F32).rearrange("q (n u) -> q n u", u=2), in_=ps[:, 0].rearrange("q u n -> q n u"))
+                nc.vector.quantize_mx(out=w2c[:].bitcast(FP8X4), scales=w2s[:], in_=gw2[:])
+
+            mx = actx.enter_context(tc.tile_pool(name="mx", bufs=2))
+            one = actx.enter_context(tc.tile_pool(name="one", bufs=1))
+
+            g1, c1, s1, g2, c2, s2, ps2, xs, xc, y0 = {}, {}, {}, {}, {}, {}, {}, {}, {}, {}
+
+            def turn(c):
+                g1[c] = mx.tile([P, 4 * HID], BF16, name="g1", tag="g1", align_bytes=64)
+                g1w = g1[c][:].bitcast(F32).rearrange("q (t b u) -> q t b u", t=TPC, u=2)
+                for half in range(2):
+                    ps = ps_tr.tile([P, 2, 2, P], F32, name="ps_h1", tag="tr")
+                    for i in range(2):
+                        words_t(ps[:, i], h1c[c][:, 2 * half + i, :])
+                    if c == 0 and half == 0:
+                        nc.vector.tensor_copy(out=g1w[:, 0:2], in_=ps[:].rearrange("q t u b -> q t b u"))
+                    else:
+                        nc.scalar.copy(out=g1w[:, 2 * half : 2 * half + 2], in_=ps[:].rearrange("q t u b -> q t b u"))
+
+            def quant1(c):
+                c1[c] = mx.tile([P, HID], U32, name="c1", tag="c1", align_bytes=64)
+                s1[c] = mx.tile([P, HID], U8, name="s1", tag="s1", align_bytes=64)
+                nc.vector.quantize_mx(out=c1[c][:].bitcast(FP8X4), scales=s1[c][:], in_=g1[c][:])
+
+            def stage1(c):
+                hc = mx.tile([P, 4, HID], BF16, name="hc", tag="hc")
+                for t in range(4):
+                    bank = ps_s1.tile([P, HID], BANK_DT, name="bank", tag="s1")
+                    nc.tensor.matmul_mx(
+                        out=bank[:],
+                        lhsT=w1c[:, t * P : (t + 1) * P].bitcast(FP8X4),
+                        lhsT_scale=w1s[:, t * P : (t + 1) * P],
+                        rhs=c1[c][:].bitcast(FP8X4),
+                        rhs_scale=s1[c][:],
+                        start=True,
+                        stop=True,
+                    )
+                    nc.scalar.activation(out=hc[:, t, :], in_=bank[:], func=ACT.Relu, bias=b1f[:, t : t + 1], scale=1.0)
+                g2[c] = mx.tile([P, 4 * HID], BF16, name="g2", tag="g2", align_bytes=64)
+                if c in V_INTERLEAVES:
+                    nc.vector.tensor_copy(out=g2[c][:].rearrange("q (b t) -> q b t", t=4), in_=hc[:].rearrange("q t b -> q b t"))
+                else:
+                    nc.scalar.copy(out=g2[c][:].rearrange("q (b t) -> q b t", t=4), in_=hc[:].rearrange("q t b -> q b t"))
+
+            def quant2(c):
+                c2[c] = mx.tile([P, HID], U32, name="c2", tag="c2", align_bytes=64)
+                s2[c] = mx.tile([P, HID], U8, name="s2", tag="s2", align_bytes=64)
+                nc.vector.quantize_mx(out=c2[c][:].bitcast(FP8X4), scales=s2[c][:], in_=g2[c][:])
+                ps2[c] = ps_s2.tile([P, TPC, NOUT], F32, name="ps2", tag="s2")
+                for i in range(TPC):
+                    nc.tensor.matmul_mx(
+                        out=ps2[c][:, i, :],
+                        lhsT=c2[c][:, i * P : (i + 1) * P].bitcast(FP8X4),
+                        lhsT_scale=s2[c][:, i * P : (i + 1) * P],
+                        rhs=w2c[:].bitcast(FP8X4),
+                        rhs_scale=w2s[:],
+                        start=True,
+                        stop=True,
+                    )
+
+            def make_x(c):
+                lo, hi = c * TPC, (c + 1) * TPC
+                xs[c] = mx.tile([P, TPC, NOUT], F32, name="xs", tag="xs")
+                xc[c] = mx.tile([P, TPC, NOUT], F32, name="xc", tag="xc")
+                for i in range(TPC):
+                    stt(xs[c][:, i, :], ps2[c][:, i, :], nrf[:, lo + i : lo + i + 1], bnr[:, lo + i, :])
+                nc.vector.tensor_scalar(out=xc[c][:], in0=xs[c][:], scalar1=-2.0, scalar2=2.0, op0=ALU.max, op1=ALU.min)
+                nc.sync.dma_start(out=x_out[:, lo:hi, :], in_=xs[c][:])
+                nc.sync.dma_start(out=xc_out[:, lo:hi, :], in_=xc[c][:])
+
+            def lay_a(c):
+                if c >= NVCH:
+                    psx = ps_tt.tile([P, TPC, P], F32, name="psx", tag="tt")
+                    for i in range(TPC):
+                        nc.tensor.transpose(psx[:, i, :], xs[c][:, i, :], ident_f[:])
+                    nc.scalar.copy(out=xT[:, (c - NVCH) * TPC : (c - NVCH + 1) * TPC, :], in_=psx[:])
+                if c < NVCH:
+                    y0[c] = mx.tile([P, NOUT, 2 * TPC], F32, name="y0", tag="y0")
+                    nc.scalar.copy(out=y0[c][:, :, 0:TPC], in_=xc[c][:].rearrange("p t n -> p n t"))
+                    nc.scalar.copy(out=y0[c][:, :, TPC : 2 * TPC], in_=xs[c][:].rearrange("p t n -> p n t"))
+                else:
+                    y0[c] = mx.tile([P, NOUT, TPC], F32, name="y0", tag="y0")
+                    nc.scalar.copy(out=y0[c][:], in_=xc[c][:].rearrange("p t n -> p n t"))
+
+            def lay_b(c):
+                lo = c * TPC
+                for i in range(TPC):
+                    sq = mx.tile([P, NOUT], F32, name="sq", tag="sq")
+                    nc.scalar.activation(out=sq[:], in_=xs[c][:, i, :], func=ACT.Square, accum_out=r0[:, lo + i : lo + i + 1])
+                    sq = mx.tile([P, NOUT], F32, name="sq", tag="sq")
+                    nc.scalar.activation(out=sq[:], in_=xc[c][:, i, :], func=ACT.Square, accum_out=r0[:, NT + lo + i : NT + lo + i + 1])
+
+            ea_re, ea_im, eb_re, eb_im = {}, {}, {}, {}
+            half = NOUT // 2
+            th0 = levels[0][0] / 2
+
+            def width(g):
+                return 2 * TPC if g < NVCH else TPC
+
+            def lane0(g):
+                return 2 * TPC * g if g < NVCH else TAIL0 + TPC * (g - NVCH)
+
+            def early_im(g):
+                ea_im[g] = one.tile([P, NOUT, width(g)], F32, name="ea_im", tag="ea_im", bufs=2)
+                b0 = y0[g][:, half:NOUT, :]
+                nc.scalar.activation(out=ea_im[g][:, 0:half, :], in_=b0, func=ACT.Copy, scale=math.sin(th0))
+                nc.scalar.activation(out=ea_im[g][:, half:NOUT, :], in_=b0, func=ACT.Copy, scale=-math.sin(th0))
+
+            def early_01(g):
+                ea_re[g] = one.tile([P, NOUT, width(g)], F32, name="ea_re", tag="ea_re")
+                eb_re[g] = one.tile([P, NOUT, width(g)], F32, name="eb_re", tag="eb_re")
+                eb_im[g] = one.tile([P, NOUT, width(g)], F32, name="eb_im", tag="eb_im")
+                a0, b0 = y0[g][:, 0:half, :], y0[g][:, half:NOUT, :]
+                stt(ea_re[g][:, 0:half, :], b0, math.cos(th0), a0)
+                stt(ea_re[g][:, half:NOUT, :], b0, -math.cos(th0), a0)
+                stage(1, ea_re[g][:], ea_im[g][:], eb_re[g][:], eb_im[g][:], True, list(range(2)))
+
+            def early_2(g):
+                stage(2, eb_re[g][:], eb_im[g][:], ea_re[g][:], ea_im[g][:], True, list(range(4)))
+
+            def early_3(g):
+                lanes = slice(lane0(g), lane0(g) + width(g))
+                stage(3, ea_re[g][:], ea_im[g][:], gb_re[:, :, lanes], gb_im[:, :, lanes], False, list(range(8)))
+
+            def live(c):
+                return 0 <= c < NCH
+
+            def tables():
+                ki = one.tile([P, 1], I32, name="ki")
+                nc.gpsimd.iota(ki[:], pattern=[[0, 1]], base=P - 1, channel_multiplier=-1)
+                kf = one.tile([P, 1], F32, name="kf")
+                nc.vector.tensor_copy(out=kf[:], in_=ki[:])
+                mrow = one.tile([P, NOUT], F32, name="mrow")
+                nc.vector.memset(mrow[:, 0:1], -1.0)
+                for n in range(NSTAGE):
+                    w = 1 << n
+                    nc.vector.tensor_scalar(out=mrow[:, w : 2 * w], in0=mrow[:, 0:w], scalar1=float(4 << (NSTAGE - 1 - n)), scalar2=None, op0=ALU.add)
+                aa = one.tile([P, 2 * NOUT], F32, name="aa")
+                nc.vector.tensor_scalar(out=aa[:, 0:NOUT], in0=mrow[:], scalar1=kf[:, 0:1], scalar2=None, op0=ALU.mult)
+                nc.vector.tensor_scalar(out=aa[:, NOUT : 2 * NOUT], in0=mrow[:], scalar1=kf[:, 0:1], scalar2=-128.0, op0=ALU.mult, op1=ALU.add)
+                ai = one.tile([P, 2 * NOUT], I32, name="ai")
+                nc.vector.tensor_copy(out=ai[:], in_=aa[:])
+                am = one.tile([P, 2 * NOUT], I32, name="am")
+                nc.vector.tensor_scalar(out=am[:], in0=ai[:], scalar1=511, scalar2=None, op0=ALU.bitwise_and)
+                xf = one.tile([P, 2 * NOUT], F32, name="xf")
+                nc.vector.tensor_scalar(out=xf[:], in0=am[:], scalar1=-256.0, scalar2=None, op0=ALU.add)
+                xa = one.tile([P, 2 * NOUT], F32, name="xa")
+                nc.scalar.activation(out=xa[:], in_=xf[:], func=ACT.Abs)
+                nc.scalar.activation(out=cs[:], in_=xa[:], func=ACT.Sin, scale=math.pi / 256, bias=-math.pi / 2)
+
+
+            for r in range(NCH + 2):
+                if 3 <= r + 2 < NCH:
+                    load(r + 2)
+                if live(r - 2):
+                    make_x(r - 2)
+                if live(r - 2):
+                    lay_a(r - 2)
+                    early_im(r - 2)
+                if live(r - 3):
+                    early_3(r - 3)
+                if live(r):
+                    turn(r)
+                if live(r - 2):
+                    early_01(r - 2)
+                if live(r - 1):
+                    stage1(r - 1)
+                if live(r):
+                    quant1(r)
+                if live(r - 1):
+                    quant2(r - 1)
+                if r == 1:
+                    tables()
+                    nc.gpsimd.memset(tpad[:], 0.0)
+                    nc.sync.dma_start(out=tpad[:, :, 0:NLAG], in_=T.rearrange("(p t) c -> p t c", t=NT))
+                    nc.gpsimd.memset(ones[:], 1.0)
+                if live(r - 2):
+                    early_2(r - 2)
+                    lay_b(r - 2)
+            early_3(NCH - 1)
+
+        with ExitStack() as bctx:
+            late = bctx.enter_context(tc.tile_pool(name="late", bufs=1))
+            two = bctx.enter_context(tc.tile_pool(name="two", bufs=2))
+            ps_fin = bctx.enter_context(tc.psum_pool(name="ps_fin", bufs=1))
+            ps_tp = bctx.enter_context(tc.psum_pool(name="ps_tp", bufs=2))
+            ps_th = bctx.enter_context(tc.psum_pool(name="ps_th", bufs=2))
+            thoff = late.tile([P, NT - TPC * NVCH, NOUT], F32, name="thoff")
+            for c in range(NCH):
+                lo, hi = c * TPC, (c + 1) * TPC
+                pst = ps_tp.tile([P, TPC, P], BF16, name="pst", tag="tp")
+                for i in range(TPC):
+                    nc.tensor.transpose(pst[:, i, :], tpad[:, lo + i, :], ident_b[:])
+                tT = two.tile([P, TPC, P], F32, name="tT", tag="tT")
+                nc.scalar.copy(out=tT[:], in_=pst[:])
+                pth = ps_th.tile([P, TPC, NOUT], F32, name="pth", tag="th")
+                for i in range(TPC):
+                    nc.tensor.matmul(out=pth[:, i, :], lhsT=tT[:, i, :], rhs=cs[:, 0:NOUT], start=True, stop=True)
+                nc.scalar.activation(out=th2[:, :, lo:hi], in_=pth[:].rearrange("p t f -> p f t"), func=ACT.Copy, scale=-2.0)
+                if c >= NVCH:
+                    nc.scalar.activation(out=thoff[:, lo - TPC * NVCH : hi - TPC * NVCH, :], in_=pth[:], func=ACT.Copy, scale=-2.0)
+            ps_of = bctx.enter_context(tc.psum_pool(name="ps_of", bufs=2))
+            sqo = late.tile([P, NT - TPC * NVCH, 2 * NOUT], F32, name="sqo")
+            for j in range((NT - TPC * NVCH) // 2):
+                pof = ps_of.tile([P, 2, 2 * NOUT], F32, name="pof", tag="of")
+                for i in range(2):
+                    nc.tensor.matmul(out=pof[:, i, :], lhsT=xT[:, 2 * j + i, :], rhs=cs[:], start=True, stop=True)
+                nc.scalar.activation(out=sqo[:, 2 * j : 2 * j + 2, :], in_=pof[:], func=ACT.Square)
+            q0 = late.tile([P, 2], F32, name="q0")
+            r0sq = late.tile([P, 2 * NT], F32, name="r0sq")
+            for y in range(2):
+                nc.scalar.activation(out=r0sq[:, y * NT : (y + 1) * NT], in_=r0[:, y * NT : (y + 1) * NT], func=ACT.Square, accum_out=q0[:, y : y + 1])
+            ga_re = late.tile([P, NOUT, LANES], F32, name="ga_re")
+            ga_im = late.tile([P, NOUT, LANES], F32, name="ga_im")
+            stage(4, gb_re[:], gb_im[:], ga_re[:], ga_im[:], True, list(range(16)))
+            stage(5, ga_re[:], ga_im[:], gb_re[:], gb_im[:], True, list(range(32)))
+            poff = late.tile([P, NT - TPC * NVCH, NOUT], F32, name="poff")
+            nc.vector.tensor_tensor(out=poff[:], in0=sqo[:, :, 0:NOUT], in1=sqo[:, :, NOUT : 2 * NOUT], op=ALU.add)
+            nc.vector.tensor_tensor(out=thoff[:], in0=thoff[:], in1=poff[:], op=ALU.add)
+            nc.scalar.activation(out=poff[:], in_=thoff[:], func=ACT.Square, accum_out=acc[:, 0, NPIECE : NPIECE + 1])
+            q0h = late.tile([P, 2], F32, name="q0h")
+            nc.vector.tensor_scalar(out=q0h[:], in0=q0[:], scalar1=0.5, scalar2=None, op0=ALU.mult)
+
+            def blocks(t, fr, y):
+                return t[:, fr, 0:TAIL0].rearrange("p f (c y i) -> p f c y i", y=2, i=TPC)[:, :, :, y, :]
+
+            npn = 64 // NPIECE
+            for k in range(NPIECE + 1):
+                if k < NPIECE:
+                    fr = slice(k * FP, (k + 1) * FP)
+                    stage(6, gb_re[:], gb_im[:], ga_re[:], ga_im[:], True, list(range(k * npn, (k + 1) * npn)))
+                    nc.scalar.activation(out=gb_re[:, fr, :], in_=ga_re[:, fr, :], func=ACT.Square)
+                    nc.scalar.activation(out=gb_im[:, fr, :], in_=ga_im[:, fr, :], func=ACT.Square)
+                if k >= 1:
+                    fr = slice((k - 1) * FP, k * FP)
+                    nc.vector.tensor_tensor(out=gb_re[:, fr, :], in0=gb_re[:, fr, :], in1=gb_im[:, fr, :], op=ALU.add)
+                    thb = th2[:, fr, 0 : TPC * NVCH].rearrange("p f (c i) -> p f c i", i=TPC)
+                    for y in range(2):
+                        nc.vector.tensor_tensor(out=blocks(gb_im, fr, y), in0=blocks(gb_re, fr, y), in1=thb, op=ALU.add)
+                    nc.vector.tensor_tensor(out=gb_im[:, fr, TAIL0:LANES], in0=gb_re[:, fr, TAIL0:LANES], in1=th2[:, fr, TPC * NVCH : NT], op=ALU.add)
+                    nc.scalar.activation(out=blocks(ga_re, fr, 1), in_=blocks(gb_im, fr, 1), func=ACT.Square, accum_out=acc[:, 0, k - 1 : k])
+                    nc.scalar.activation(out=blocks(ga_re, fr, 0), in_=blocks(gb_im, fr, 0), func=ACT.Square, accum_out=acc[:, 1, k - 1 : k])
+                    nc.scalar.activation(out=ga_re[:, fr, TAIL0:LANES], in_=gb_im[:, fr, TAIL0:LANES], func=ACT.Square, accum_out=acc[:, 1, NPIECE + k - 1 : NPIECE + k])
+
+            sd = late.tile([P, 2], F32, name="sd")
+            nc.vector.tensor_reduce(out=sd[:], in_=acc[:], axis=AX.X, op=ALU.add)
+            part = late.tile([P, 2], F32, name="part")
+            stt(part[:], sd[:], 1.0 / 256.0, q0h[:], ALU.subtract)
+            pfin = ps_fin.tile([P, 2], F32, name="pfin")
+            nc.tensor.matmul(out=pfin[:], lhsT=ones[:], rhs=part[:], start=True, stop=True)
+            res = late.tile([P, 2], F32, name="res")
+            nc.scalar.activation(out=res[:], in_=pfin[:], func=ACT.Copy, scale=1.0 / (ROWS * NLAG))
+            nc.sync.dma_start(out=out_1.rearrange("(a b) -> a b", a=1), in_=res[0:1, 0:1])
+            nc.sync.dma_start(out=out_3.rearrange("(a b) -> a b", a=1), in_=res[0:1, 1:2])

@@ -21,14 +21,12 @@ ROWS, HID, NOUT, NLAG = 4096, 512, 128, 127
 NT = ROWS // P
 TPC = 4
 NCH = NT // TPC
-NVCH = 5
-TAIL0 = 2 * TPC * NVCH
-LANES = TAIL0 + TPC * (NCH - NVCH)
+NVCH = 4
+NSG = NVCH + NCH
 NSTAGE = 7
 NEARLY = 4
 NPIECE = 8
 V_INTERLEAVES = (0, 1)
-FP = NOUT // NPIECE
 
 FLOPS = 2 * ROWS * HID * HID + 2 * ROWS * HID * NOUT
 
@@ -47,35 +45,44 @@ def tile_qdtssolveronnx_pa_kernel(tc, h1, w_hid2, b_hid2, w_out, b_out, norm_roo
     xc_out = out_2.rearrange("(p t) n -> p t n", t=NT)
     levels = tree_levels()
 
+    def nsg(c):
+        return 2 if c < NVCH else 1
+
+    def sg0(c):
+        return 2 * c if c < NVCH else NVCH + c
+
     def stt(out, in0, scalar, in1, op1=ALU.add):
         nc.vector.scalar_tensor_tensor(out=out, in0=in0, scalar=scalar, in1=in1, op0=ALU.mult, op1=op1)
 
-    def stage(s, sr, si, dr, di, merged, nodes):
+    def both(z, g0, g1):
+        return z[:].rearrange("p g c n w -> p (g c) n w")[:, 2 * g0 : 2 * g1]
+
+    def halves(i, size):
+        return slice(i * size, i * size + size // 2), slice(i * size + size // 2, (i + 1) * size)
+
+    def plus(s, src, dst, g0, g1, nodes):
         size = NOUT >> s
-        h = size // 2
         rs = [(math.cos(v / 2), math.sin(v / 2)) for v in levels[s]]
-        for which in range(4):
-            for i in nodes:
-                rr, ri = rs[i]
-                top, bot = slice(i * size, i * size + h), slice(i * size + h, (i + 1) * size)
-                if which == 0:
-                    stt(dr[:, top, :], sr[:, bot, :], rr, sr[:, top, :])
-                elif which == 1:
-                    stt(di[:, top, :], si[:, bot, :], rr, si[:, top, :])
-                elif which == 2:
-                    stt(dr[:, top, :], si[:, bot, :], -ri, dr[:, top, :])
-                else:
-                    stt(di[:, top, :], sr[:, bot, :], ri, di[:, top, :])
-        for a, d in ((sr, dr), (si, di)):
-            if merged:
-                rows = slice(nodes[0] * size, (nodes[-1] + 1) * size)
-                av = a[:, rows, :].rearrange("p (i c j) l -> p i c (j l)", c=2, j=h)
-                dv = d[:, rows, :].rearrange("p (i c j) l -> p i c (j l)", c=2, j=h)
-                stt(dv[:, :, 1, :], av[:, :, 0, :], 2.0, dv[:, :, 0, :], ALU.subtract)
-            else:
-                for i in nodes:
-                    top, bot = slice(i * size, i * size + h), slice(i * size + h, (i + 1) * size)
-                    stt(d[:, bot, :], a[:, top, :], 2.0, d[:, top, :], ALU.subtract)
+        sv, dv = both(src, g0, g1), both(dst, g0, g1)
+        for i in nodes:
+            top, bot = halves(i, size)
+            stt(dv[:, :, top, :], sv[:, :, bot, :], rs[i][0], sv[:, :, top, :])
+        for i in nodes:
+            top, bot = halves(i, size)
+            stt(dst[:, g0:g1, 0, top, :], src[:, g0:g1, 1, bot, :], -rs[i][1], dst[:, g0:g1, 0, top, :])
+        for i in nodes:
+            top, bot = halves(i, size)
+            stt(dst[:, g0:g1, 1, top, :], src[:, g0:g1, 0, bot, :], rs[i][1], dst[:, g0:g1, 1, top, :])
+
+    def minus(s, src, dst, g0, g1):
+        h = NOUT >> (s + 1)
+        av = both(src, g0, g1).rearrange("p a (i k j) w -> p (a i) k (j w)", k=2, j=h)
+        dv = both(dst, g0, g1).rearrange("p a (i k j) w -> p (a i) k (j w)", k=2, j=h)
+        stt(dv[:, :, 1, :], av[:, :, 0, :], 2.0, dv[:, :, 0, :], ALU.subtract)
+
+    def stage(s, src, dst, g0, g1):
+        plus(s, src, dst, g0, g1, list(range(1 << s)))
+        minus(s, src, dst, g0, g1)
 
     with ExitStack() as ctx:
         assert NCH * TPC == NT
@@ -85,9 +92,13 @@ def tile_qdtssolveronnx_pa_kernel(tc, h1, w_hid2, b_hid2, w_out, b_out, norm_roo
         make_identity(nc, ident_f[:])
         ident_b = keep.tile([P, P], BF16, name="ident_b")
         make_identity(nc, ident_b[:])
-        ones = keep.tile([P, P], F32, name="ones")
+        wide = keep.tile([P, P], F32, name="wide")
+        nc.gpsimd.memset(wide[:], 0.0)
         tpad = keep.tile([P, NT, P], BF16, name="tpad")
+        nc.gpsimd.memset(tpad[:], 0.0)
 
+        ki = keep.tile([P, 1], I32, name="ki")
+        nc.gpsimd.iota(ki[:], pattern=[[0, 1]], base=P - 1, channel_multiplier=-1)
         cs = keep.tile([P, 2 * NOUT], F32, name="cs")
         w1c = keep.tile([P, HID], U32, name="w1c", align_bytes=64)
         w1s = keep.tile([P, HID], U8, name="w1s", align_bytes=64)
@@ -95,14 +106,13 @@ def tile_qdtssolveronnx_pa_kernel(tc, h1, w_hid2, b_hid2, w_out, b_out, norm_roo
         w2s = keep.tile([P, NOUT], U8, name="w2s", align_bytes=64)
         b1f = keep.tile([P, 4], F32, name="b1f")
         nrf = keep.tile([P, NT], F32, name="nrf")
-        bnr = keep.tile([P, NT, NOUT], F32, name="bnr")
+        bof = keep.tile([P, NOUT], F32, name="bof")
         xT = keep.tile([P, NT - TPC * NVCH, P], F32, name="xT")
-        th2 = keep.tile([P, NOUT, NT], F32, name="th2")
         r0 = keep.tile([P, 2 * NT], F32, name="r0")
-        acc = keep.tile([P, 2, 2 * NPIECE], F32, name="acc")
+        acc = keep.tile([P, 2, 8], F32, name="acc")
         nc.vector.memset(acc[:], 0.0)
-        gb_re = keep.tile([P, NOUT, LANES], F32, name="gb_re")
-        gb_im = keep.tile([P, NOUT, LANES], F32, name="gb_im")
+        za = keep.tile([P, NSG, 2, NOUT, TPC], F32, name="za")
+        zb = keep.tile([P, NSG, 2, NOUT, TPC], F32, name="zb")
 
         def words_t(ps, src):
             words = src.bitcast(F32)
@@ -135,11 +145,11 @@ def tile_qdtssolveronnx_pa_kernel(tc, h1, w_hid2, b_hid2, w_out, b_out, norm_roo
                 nc.sync.dma_start(out=boraw[:], in_=b_out.partition_broadcast(P))
                 load(1)
                 load(2)
+                nc.sync.dma_start(out=tpad[:, :, 0:NLAG], in_=T.rearrange("(p t) c -> p t c", t=NT))
 
                 nc.vector.tensor_copy(out=b1f[:], in_=b1raw[:])
                 nc.vector.tensor_copy(out=nrf[:], in_=nrraw[:])
-                for tau in range(NT):
-                    nc.gpsimd.tensor_scalar(out=bnr[:, tau, :], in0=boraw[:], scalar1=nrf[:, tau : tau + 1], scalar2=0.0, op0=ALU.mult, op1=ALU.add)
+                nc.vector.tensor_copy(out=bof[:], in_=boraw[:])
 
                 gw1 = pre.tile([P, 4 * HID], BF16, name="gw1", align_bytes=64)
                 gw1w = gw1[:].bitcast(F32).rearrange("q (t m u) -> q t m u", t=4, u=2)
@@ -194,12 +204,22 @@ def tile_qdtssolveronnx_pa_kernel(tc, h1, w_hid2, b_hid2, w_out, b_out, norm_roo
                         start=True,
                         stop=True,
                     )
-                    nc.scalar.activation(out=hc[:, t, :], in_=bank[:], func=ACT.Relu, bias=b1f[:, t : t + 1], scale=1.0)
+                    if c == 0 and t >= 2:
+                        nc.vector.tensor_scalar(out=hc[:, t, :], in0=bank[:], scalar1=b1f[:, t : t + 1], scalar2=0.0, op0=ALU.add, op1=ALU.max)
+                    else:
+                        nc.scalar.activation(out=hc[:, t, :], in_=bank[:], func=ACT.Relu, bias=b1f[:, t : t + 1], scale=1.0)
                 g2[c] = mx.tile([P, 4 * HID], BF16, name="g2", tag="g2", align_bytes=64)
                 if c in V_INTERLEAVES:
                     nc.vector.tensor_copy(out=g2[c][:].rearrange("q (b t) -> q b t", t=4), in_=hc[:].rearrange("q t b -> q b t"))
                 else:
                     nc.scalar.copy(out=g2[c][:].rearrange("q (b t) -> q b t", t=4), in_=hc[:].rearrange("q t b -> q b t"))
+
+            bnr = {}
+
+            def bias_rows(c):
+                bnr[c] = mx.tile([P, TPC, NOUT], F32, name="bnr", tag="bnr")
+                for i in range(TPC):
+                    nc.scalar.activation(out=bnr[c][:, i, :], in_=bof[:], func=ACT.Copy, scale=nrf[:, c * TPC + i : c * TPC + i + 1])
 
             def quant2(c):
                 c2[c] = mx.tile([P, HID], U32, name="c2", tag="c2", align_bytes=64)
@@ -222,7 +242,7 @@ def tile_qdtssolveronnx_pa_kernel(tc, h1, w_hid2, b_hid2, w_out, b_out, norm_roo
                 xs[c] = mx.tile([P, TPC, NOUT], F32, name="xs", tag="xs")
                 xc[c] = mx.tile([P, TPC, NOUT], F32, name="xc", tag="xc")
                 for i in range(TPC):
-                    stt(xs[c][:, i, :], ps2[c][:, i, :], nrf[:, lo + i : lo + i + 1], bnr[:, lo + i, :])
+                    stt(xs[c][:, i, :], ps2[c][:, i, :], nrf[:, lo + i : lo + i + 1], bnr[c][:, i, :])
                 nc.vector.tensor_scalar(out=xc[c][:], in0=xs[c][:], scalar1=-2.0, scalar2=2.0, op0=ALU.max, op1=ALU.min)
                 nc.sync.dma_start(out=x_out[:, lo:hi, :], in_=xs[c][:])
                 nc.sync.dma_start(out=xc_out[:, lo:hi, :], in_=xc[c][:])
@@ -233,13 +253,10 @@ def tile_qdtssolveronnx_pa_kernel(tc, h1, w_hid2, b_hid2, w_out, b_out, norm_roo
                     for i in range(TPC):
                         nc.tensor.transpose(psx[:, i, :], xs[c][:, i, :], ident_f[:])
                     nc.scalar.copy(out=xT[:, (c - NVCH) * TPC : (c - NVCH + 1) * TPC, :], in_=psx[:])
+                y0[c] = mx.tile([P, nsg(c), NOUT, TPC], F32, name="y0", tag="y0")
+                nc.scalar.copy(out=y0[c][:, 0], in_=xc[c][:].rearrange("p t n -> p n t"))
                 if c < NVCH:
-                    y0[c] = mx.tile([P, NOUT, 2 * TPC], F32, name="y0", tag="y0")
-                    nc.scalar.copy(out=y0[c][:, :, 0:TPC], in_=xc[c][:].rearrange("p t n -> p n t"))
-                    nc.scalar.copy(out=y0[c][:, :, TPC : 2 * TPC], in_=xs[c][:].rearrange("p t n -> p n t"))
-                else:
-                    y0[c] = mx.tile([P, NOUT, TPC], F32, name="y0", tag="y0")
-                    nc.scalar.copy(out=y0[c][:], in_=xc[c][:].rearrange("p t n -> p n t"))
+                    nc.scalar.copy(out=y0[c][:, 1], in_=xs[c][:].rearrange("p t n -> p n t"))
 
             def lay_b(c):
                 lo = c * TPC
@@ -249,44 +266,33 @@ def tile_qdtssolveronnx_pa_kernel(tc, h1, w_hid2, b_hid2, w_out, b_out, norm_roo
                     sq = mx.tile([P, NOUT], F32, name="sq", tag="sq")
                     nc.scalar.activation(out=sq[:], in_=xc[c][:, i, :], func=ACT.Square, accum_out=r0[:, NT + lo + i : NT + lo + i + 1])
 
-            ea_re, ea_im, eb_re, eb_im = {}, {}, {}, {}
             half = NOUT // 2
             th0 = levels[0][0] / 2
 
-            def width(g):
-                return 2 * TPC if g < NVCH else TPC
+            def early_im(c):
+                g0, g1 = sg0(c), sg0(c) + nsg(c)
+                b0 = y0[c][:, :, half:NOUT, :]
+                nc.scalar.activation(out=za[:, g0:g1, 1, 0:half, :], in_=b0, func=ACT.Copy, scale=math.sin(th0))
+                nc.scalar.activation(out=za[:, g0:g1, 1, half:NOUT, :], in_=b0, func=ACT.Copy, scale=-math.sin(th0))
 
-            def lane0(g):
-                return 2 * TPC * g if g < NVCH else TAIL0 + TPC * (g - NVCH)
+            def early_01(c):
+                g0, g1 = sg0(c), sg0(c) + nsg(c)
+                a0, b0 = y0[c][:, :, 0:half, :], y0[c][:, :, half:NOUT, :]
+                stt(za[:, g0:g1, 0, 0:half, :], b0, math.cos(th0), a0)
+                stt(za[:, g0:g1, 0, half:NOUT, :], b0, -math.cos(th0), a0)
+                stage(1, za, zb, g0, g1)
 
-            def early_im(g):
-                ea_im[g] = one.tile([P, NOUT, width(g)], F32, name="ea_im", tag="ea_im", bufs=2)
-                b0 = y0[g][:, half:NOUT, :]
-                nc.scalar.activation(out=ea_im[g][:, 0:half, :], in_=b0, func=ACT.Copy, scale=math.sin(th0))
-                nc.scalar.activation(out=ea_im[g][:, half:NOUT, :], in_=b0, func=ACT.Copy, scale=-math.sin(th0))
+            def early_2(c):
+                stage(2, zb, za, sg0(c), sg0(c) + nsg(c))
 
-            def early_01(g):
-                ea_re[g] = one.tile([P, NOUT, width(g)], F32, name="ea_re", tag="ea_re")
-                eb_re[g] = one.tile([P, NOUT, width(g)], F32, name="eb_re", tag="eb_re")
-                eb_im[g] = one.tile([P, NOUT, width(g)], F32, name="eb_im", tag="eb_im")
-                a0, b0 = y0[g][:, 0:half, :], y0[g][:, half:NOUT, :]
-                stt(ea_re[g][:, 0:half, :], b0, math.cos(th0), a0)
-                stt(ea_re[g][:, half:NOUT, :], b0, -math.cos(th0), a0)
-                stage(1, ea_re[g][:], ea_im[g][:], eb_re[g][:], eb_im[g][:], True, list(range(2)))
-
-            def early_2(g):
-                stage(2, eb_re[g][:], eb_im[g][:], ea_re[g][:], ea_im[g][:], True, list(range(4)))
-
-            def early_3(g):
-                lanes = slice(lane0(g), lane0(g) + width(g))
-                stage(3, ea_re[g][:], ea_im[g][:], gb_re[:, :, lanes], gb_im[:, :, lanes], False, list(range(8)))
+            def early_3(c):
+                if NEARLY > 3:
+                    stage(3, za, zb, sg0(c), sg0(c) + nsg(c))
 
             def live(c):
                 return 0 <= c < NCH
 
             def tables():
-                ki = one.tile([P, 1], I32, name="ki")
-                nc.gpsimd.iota(ki[:], pattern=[[0, 1]], base=P - 1, channel_multiplier=-1)
                 kf = one.tile([P, 1], F32, name="kf")
                 nc.vector.tensor_copy(out=kf[:], in_=ki[:])
                 mrow = one.tile([P, NOUT], F32, name="mrow")
@@ -327,12 +333,10 @@ def tile_qdtssolveronnx_pa_kernel(tc, h1, w_hid2, b_hid2, w_out, b_out, norm_roo
                 if live(r):
                     quant1(r)
                 if live(r - 1):
+                    bias_rows(r - 1)
                     quant2(r - 1)
                 if r == 1:
                     tables()
-                    nc.gpsimd.memset(tpad[:], 0.0)
-                    nc.sync.dma_start(out=tpad[:, :, 0:NLAG], in_=T.rearrange("(p t) c -> p t c", t=NT))
-                    nc.gpsimd.memset(ones[:], 1.0)
                 if live(r - 2):
                     early_2(r - 2)
                     lay_b(r - 2)
@@ -344,7 +348,10 @@ def tile_qdtssolveronnx_pa_kernel(tc, h1, w_hid2, b_hid2, w_out, b_out, norm_roo
             ps_fin = bctx.enter_context(tc.psum_pool(name="ps_fin", bufs=1))
             ps_tp = bctx.enter_context(tc.psum_pool(name="ps_tp", bufs=2))
             ps_th = bctx.enter_context(tc.psum_pool(name="ps_th", bufs=2))
-            thoff = late.tile([P, NT - TPC * NVCH, NOUT], F32, name="thoff")
+            ps_of = bctx.enter_context(tc.psum_pool(name="ps_of", bufs=2))
+            noff = NT - TPC * NVCH
+            th2 = late.tile([P, NCH, NOUT, TPC], F32, name="th2")
+            thoff = late.tile([P, noff, NOUT], F32, name="thoff")
             for c in range(NCH):
                 lo, hi = c * TPC, (c + 1) * TPC
                 pst = ps_tp.tile([P, TPC, P], BF16, name="pst", tag="tp")
@@ -355,12 +362,11 @@ def tile_qdtssolveronnx_pa_kernel(tc, h1, w_hid2, b_hid2, w_out, b_out, norm_roo
                 pth = ps_th.tile([P, TPC, NOUT], F32, name="pth", tag="th")
                 for i in range(TPC):
                     nc.tensor.matmul(out=pth[:, i, :], lhsT=tT[:, i, :], rhs=cs[:, 0:NOUT], start=True, stop=True)
-                nc.scalar.activation(out=th2[:, :, lo:hi], in_=pth[:].rearrange("p t f -> p f t"), func=ACT.Copy, scale=-2.0)
+                nc.scalar.activation(out=th2[:, c], in_=pth[:].rearrange("p t f -> p f t"), func=ACT.Copy, scale=-2.0)
                 if c >= NVCH:
                     nc.scalar.activation(out=thoff[:, lo - TPC * NVCH : hi - TPC * NVCH, :], in_=pth[:], func=ACT.Copy, scale=-2.0)
-            ps_of = bctx.enter_context(tc.psum_pool(name="ps_of", bufs=2))
-            sqo = late.tile([P, NT - TPC * NVCH, 2 * NOUT], F32, name="sqo")
-            for j in range((NT - TPC * NVCH) // 2):
+            sqo = late.tile([P, noff, 2 * NOUT], F32, name="sqo")
+            for j in range(noff // 2):
                 pof = ps_of.tile([P, 2, 2 * NOUT], F32, name="pof", tag="of")
                 for i in range(2):
                     nc.tensor.matmul(out=pof[:, i, :], lhsT=xT[:, 2 * j + i, :], rhs=cs[:], start=True, stop=True)
@@ -369,45 +375,58 @@ def tile_qdtssolveronnx_pa_kernel(tc, h1, w_hid2, b_hid2, w_out, b_out, norm_roo
             r0sq = late.tile([P, 2 * NT], F32, name="r0sq")
             for y in range(2):
                 nc.scalar.activation(out=r0sq[:, y * NT : (y + 1) * NT], in_=r0[:, y * NT : (y + 1) * NT], func=ACT.Square, accum_out=q0[:, y : y + 1])
-            ga_re = late.tile([P, NOUT, LANES], F32, name="ga_re")
-            ga_im = late.tile([P, NOUT, LANES], F32, name="ga_im")
-            stage(4, gb_re[:], gb_im[:], ga_re[:], ga_im[:], True, list(range(16)))
-            stage(5, ga_re[:], ga_im[:], gb_re[:], gb_im[:], True, list(range(32)))
-            poff = late.tile([P, NT - TPC * NVCH, NOUT], F32, name="poff")
+
+            pair = [za, zb]
+            for s in range(NEARLY, NSTAGE - 1):
+                stage(s, pair[(s + 1) % 2], pair[s % 2], 0, NSG)
+            poff = late.tile([P, noff, NOUT], F32, name="poff")
             nc.vector.tensor_tensor(out=poff[:], in0=sqo[:, :, 0:NOUT], in1=sqo[:, :, NOUT : 2 * NOUT], op=ALU.add)
             nc.vector.tensor_tensor(out=thoff[:], in0=thoff[:], in1=poff[:], op=ALU.add)
-            nc.scalar.activation(out=poff[:], in_=thoff[:], func=ACT.Square, accum_out=acc[:, 0, NPIECE : NPIECE + 1])
+            nc.scalar.activation(out=poff[:], in_=thoff[:], func=ACT.Square, accum_out=acc[:, 0, 7:8])
             q0h = late.tile([P, 2], F32, name="q0h")
             nc.vector.tensor_scalar(out=q0h[:], in0=q0[:], scalar1=0.5, scalar2=None, op0=ALU.mult)
 
-            def blocks(t, fr, y):
-                return t[:, fr, 0:TAIL0].rearrange("p f (c y i) -> p f c y i", y=2, i=TPC)[:, :, :, y, :]
+            npn = (NOUT // 2) // NPIECE
+            for k in range(NPIECE):
+                plus(NSTAGE - 1, zb, za, 0, NSG, list(range(k * npn, (k + 1) * npn)))
+                rows = slice(2 * k * npn, 2 * (k + 1) * npn, 2)
+                spare = slice(2 * k * npn + 1, 2 * (k + 1) * npn, 2)
+                nc.scalar.activation(out=both(zb, 0, NSG)[:, :, spare, :], in_=both(za, 0, NSG)[:, :, rows, :], func=ACT.Square)
+            cuts = [(0, 4), (4, 8), (8, NSG)]
+            upper, bottom = slice(0, NOUT, 2), slice(1, NOUT, 2)
+            for g0, g1 in cuts:
+                minus(NSTAGE - 1, zb, za, g0, g1)
+                nc.scalar.activation(out=both(zb, g0, g1)[:, :, upper, :], in_=both(za, g0, g1)[:, :, bottom, :], func=ACT.Square)
 
-            npn = 64 // NPIECE
-            for k in range(NPIECE + 1):
-                if k < NPIECE:
-                    fr = slice(k * FP, (k + 1) * FP)
-                    stage(6, gb_re[:], gb_im[:], ga_re[:], ga_im[:], True, list(range(k * npn, (k + 1) * npn)))
-                    nc.scalar.activation(out=gb_re[:, fr, :], in_=ga_re[:, fr, :], func=ACT.Square)
-                    nc.scalar.activation(out=gb_im[:, fr, :], in_=ga_im[:, fr, :], func=ACT.Square)
-                if k >= 1:
-                    fr = slice((k - 1) * FP, k * FP)
-                    nc.vector.tensor_tensor(out=gb_re[:, fr, :], in0=gb_re[:, fr, :], in1=gb_im[:, fr, :], op=ALU.add)
-                    thb = th2[:, fr, 0 : TPC * NVCH].rearrange("p f (c i) -> p f c i", i=TPC)
-                    for y in range(2):
-                        nc.vector.tensor_tensor(out=blocks(gb_im, fr, y), in0=blocks(gb_re, fr, y), in1=thb, op=ALU.add)
-                    nc.vector.tensor_tensor(out=gb_im[:, fr, TAIL0:LANES], in0=gb_re[:, fr, TAIL0:LANES], in1=th2[:, fr, TPC * NVCH : NT], op=ALU.add)
-                    nc.scalar.activation(out=blocks(ga_re, fr, 1), in_=blocks(gb_im, fr, 1), func=ACT.Square, accum_out=acc[:, 0, k - 1 : k])
-                    nc.scalar.activation(out=blocks(ga_re, fr, 0), in_=blocks(gb_im, fr, 0), func=ACT.Square, accum_out=acc[:, 1, k - 1 : k])
-                    nc.scalar.activation(out=ga_re[:, fr, TAIL0:LANES], in_=gb_im[:, fr, TAIL0:LANES], func=ACT.Square, accum_out=acc[:, 1, NPIECE + k - 1 : NPIECE + k])
+            cols = [0, 0]
+
+            def finish(freqs, rows, g0, g1):
+                nc.vector.tensor_tensor(out=zb[:, g0:g1, 0, rows, :], in0=zb[:, g0:g1, 0, rows, :], in1=zb[:, g0:g1, 1, rows, :], op=ALU.add)
+                e1 = min(g1, 2 * NVCH)
+                parts = []
+                if g0 < e1:
+                    parts.append((slice(g0, e1, 2), slice(g0 // 2, e1 // 2), 1))
+                    parts.append((slice(g0 + 1, e1, 2), slice(g0 // 2, e1 // 2), 0))
+                if g1 > 2 * NVCH:
+                    t0 = max(g0, 2 * NVCH)
+                    parts.append((slice(t0, g1), slice(t0 - NVCH, g1 - NVCH), 1))
+                for gs, ch, y in parts:
+                    nc.vector.tensor_tensor(out=zb[:, gs, 1, rows, :], in0=zb[:, gs, 0, rows, :], in1=th2[:, ch, freqs, :], op=ALU.add)
+                for gs, ch, y in parts:
+                    nc.scalar.activation(out=za[:, gs, 0, rows, :], in_=zb[:, gs, 1, rows, :], func=ACT.Square, accum_out=acc[:, y, cols[y] : cols[y] + 1])
+                    cols[y] += 1
+
+            finish(upper, bottom, 0, NSG)
+            for g0, g1 in cuts:
+                finish(bottom, upper, g0, g1)
 
             sd = late.tile([P, 2], F32, name="sd")
             nc.vector.tensor_reduce(out=sd[:], in_=acc[:], axis=AX.X, op=ALU.add)
-            part = late.tile([P, 2], F32, name="part")
-            stt(part[:], sd[:], 1.0 / 256.0, q0h[:], ALU.subtract)
-            pfin = ps_fin.tile([P, 2], F32, name="pfin")
-            nc.tensor.matmul(out=pfin[:], lhsT=ones[:], rhs=part[:], start=True, stop=True)
-            res = late.tile([P, 2], F32, name="res")
-            nc.scalar.activation(out=res[:], in_=pfin[:], func=ACT.Copy, scale=1.0 / (ROWS * NLAG))
+            stt(wide[:, 0:2], sd[:], 1.0 / 256.0, q0h[:], ALU.subtract)
+            pfin = ps_fin.tile([P, P], F32, name="pfin")
+            nc.tensor.transpose(pfin[:], wide[:], ident_f[:])
+            junk = late.tile([P, P], F32, name="junk")
+            res = late.tile([P, 1], F32, name="res")
+            nc.scalar.activation(out=junk[:], in_=pfin[:], func=ACT.Copy, scale=1.0 / (ROWS * NLAG), accum_out=res[:])
             nc.sync.dma_start(out=out_1.rearrange("(a b) -> a b", a=1), in_=res[0:1, 0:1])
-            nc.sync.dma_start(out=out_3.rearrange("(a b) -> a b", a=1), in_=res[0:1, 1:2])
+            nc.sync.dma_start(out=out_3.rearrange("(a b) -> a b", a=1), in_=res[1:2, 0:1])

from contextlib import ExitStack
import math

import concourse.mybir as mybir
from concourse.masks import make_identity

F32 = mybir.dt.float32
BF16 = mybir.dt.bfloat16
I32 = mybir.dt.int32
U32 = mybir.dt.uint32
U8 = mybir.dt.uint8
FP8X4 = mybir.dt.float8_e4m3fn_x4
ALU = mybir.AluOpType
ACT = mybir.ActivationFunctionType
AX = mybir.AxisListType

BANK_DT = F32

P = 128
ROWS, HID, NOUT, NLAG = 4096, 512, 128, 127
NT = ROWS // P
TPC = 4
NCH = NT // TPC
NVCH = 4
NSG = NVCH + NCH
NSTAGE = 7
NEARLY = 4
NPIECE = 8
V_INTERLEAVES = (0, 1)

FLOPS = 2 * ROWS * HID * HID + 2 * ROWS * HID * NOUT


def tree_levels():
    levels = [[-math.pi / 2]]
    for s in range(NSTAGE):
        levels.append([w for v in levels[s] for w in (v / 2, v / 2 + math.pi)])
    return levels


def tile_qdtssolveronnx_pa_kernel(tc, h1, w_hid2, b_hid2, w_out, b_out, norm_root, T, out_0, out_1, out_2, out_3):
    nc = tc.nc
    h1v = h1.rearrange("(p t) k -> p t k", t=NT)
    x_out = out_0.rearrange("(p t) n -> p t n", t=NT)
    xc_out = out_2.rearrange("(p t) n -> p t n", t=NT)
    levels = tree_levels()

    def nsg(c):
        return 2 if c < NVCH else 1

    def sg0(c):
        return 2 * c if c < NVCH else NVCH + c

    def stt(out, in0, scalar, in1, op1=ALU.add):
        nc.vector.scalar_tensor_tensor(out=out, in0=in0, scalar=scalar, in1=in1, op0=ALU.mult, op1=op1)

    def both(z, g0, g1):
        return z[:].rearrange("p g c n w -> p (g c) n w")[:, 2 * g0 : 2 * g1]

    def halves(i, size):
        return slice(i * size, i * size + size // 2), slice(i * size + size // 2, (i + 1) * size)

    def plus(s, src, dst, g0, g1, nodes):
        size = NOUT >> s
        rs = [(math.cos(v / 2), math.sin(v / 2)) for v in levels[s]]
        sv, dv = both(src, g0, g1), both(dst, g0, g1)
        for i in nodes:
            top, bot = halves(i, size)
            stt(dv[:, :, top, :], sv[:, :, bot, :], rs[i][0], sv[:, :, top, :])
        for i in nodes:
            top, bot = halves(i, size)
            stt(dst[:, g0:g1, 0, top, :], src[:, g0:g1, 1, bot, :], -rs[i][1], dst[:, g0:g1, 0, top, :])
        for i in nodes:
            top, bot = halves(i, size)
            stt(dst[:, g0:g1, 1, top, :], src[:, g0:g1, 0, bot, :], rs[i][1], dst[:, g0:g1, 1, top, :])

    def minus(s, src, dst, g0, g1):
        h = NOUT >> (s + 1)
        av = both(src, g0, g1).rearrange("p a (i k j) w -> p (a i) k (j w)", k=2, j=h)
        dv = both(dst, g0, g1).rearrange("p a (i k j) w -> p (a i) k (j w)", k=2, j=h)
        stt(dv[:, :, 1, :], av[:, :, 0, :], 2.0, dv[:, :, 0, :], ALU.subtract)

    def stage(s, src, dst, g0, g1):
        plus(s, src, dst, g0, g1, list(range(1 << s)))
        minus(s, src, dst, g0, g1)

    with ExitStack() as ctx:
        assert NCH * TPC == NT
        keep = ctx.enter_context(tc.tile_pool(name="keep", bufs=1))

        ident_f = keep.tile([P, P], F32, name="ident_f")
        make_identity(nc, ident_f[:])
        ident_b = keep.tile([P, P], BF16, name="ident_b")
        make_identity(nc, ident_b[:])
        wide = keep.tile([P, P], F32, name="wide")
        nc.gpsimd.memset(wide[:], 0.0)
        tpad = keep.tile([P, NT, P], BF16, name="tpad")
        nc.gpsimd.memset(tpad[:], 0.0)

        ki = keep.tile([P, 1], I32, name="ki")
        nc.gpsimd.iota(ki[:], pattern=[[0, 1]], base=P - 1, channel_multiplier=-1)
        cs = keep.tile([P, 2 * NOUT], F32, name="cs")
        w1c = keep.tile([P, HID], U32, name="w1c", align_bytes=64)
        w1s = keep.tile([P, HID], U8, name="w1s", align_bytes=64)
        w2c = keep.tile([P, NOUT], U32, name="w2c", align_bytes=64)
        w2s = keep.tile([P, NOUT], U8, name="w2s", align_bytes=64)
        b1f = keep.tile([P, 4], F32, name="b1f")
        nrf = keep.tile([P, NT], F32, name="nrf")
        bof = keep.tile([P, NOUT], F32, name="bof")
        xT = keep.tile([P, NT - TPC * NVCH, P], F32, name="xT")
        r0 = keep.tile([P, 2 * NT], F32, name="r0")
        acc = keep.tile([P, 2, 8], F32, name="acc")
        nc.vector.memset(acc[:], 0.0)
        za = keep.tile([P, NSG, 2, NOUT, TPC], F32, name="za")
        zb = keep.tile([P, NSG, 2, NOUT, TPC], F32, name="zb")

        def words_t(ps, src):
            words = src.bitcast(F32)
            for u in range(2):
                nc.tensor.transpose(ps[:, u, :], words[:, u : HID // 2 : 2], ident_f[:])

        with ExitStack() as actx:
            ps_tr = actx.enter_context(tc.psum_pool(name="ps_tr", bufs=2))
            ps_s1 = actx.enter_context(tc.psum_pool(name="ps_s1", bufs=4))
            ps_s2 = actx.enter_context(tc.psum_pool(name="ps_s2", bufs=1))
            ps_tt = actx.enter_context(tc.psum_pool(name="ps_tt", bufs=1))
            hp = actx.enter_context(tc.tile_pool(name="hp", bufs=3))
            h1c = {}

            def load(c):
                h1c[c] = hp.tile([P, TPC, HID], BF16, name="h1c", tag="h1c")
                nc.sync.dma_start(out=h1c[c][:], in_=h1v[:, c * TPC : (c + 1) * TPC, :])

            with tc.tile_pool(name="prep", bufs=1) as pre:
                w1raw = pre.tile([P, 4, HID], BF16, name="w1raw")
                nc.sync.dma_start(out=w1raw[:], in_=w_hid2.rearrange("(m t) k -> m t k", t=4))
                load(0)
                w2raw = pre.tile([P, HID], BF16, name="w2raw")
                nc.sync.dma_start(out=w2raw[:], in_=w_out)
                b1raw = pre.tile([P, 4], BF16, name="b1raw")
                nc.sync.dma_start(out=b1raw[:], in_=b_hid2.rearrange("(p t) -> p t", t=4))
                nrraw = pre.tile([P, NT], BF16, name="nrraw")
                nc.sync.dma_start(out=nrraw[:], in_=norm_root.rearrange("(p t) o -> p (t o)", t=NT))
                boraw = pre.tile([P, NOUT], BF16, name="boraw")
                nc.sync.dma_start(out=boraw[:], in_=b_out.partition_broadcast(P))
                load(1)
                load(2)
                nc.sync.dma_start(out=tpad[:, :, 0:NLAG], in_=T.rearrange("(p t) c -> p t c", t=NT))

                nc.vector.tensor_copy(out=b1f[:], in_=b1raw[:])
                nc.vector.tensor_copy(out=nrf[:], in_=nrraw[:])
                nc.vector.tensor_copy(out=bof[:], in_=boraw[:])

                gw1 = pre.tile([P, 4 * HID], BF16, name="gw1", align_bytes=64)
                gw1w = gw1[:].bitcast(F32).rearrange("q (t m u) -> q t m u", t=4, u=2)
                for half in range(2):
                    ps = ps_tr.tile([P, 2, 2, P], F32, name="ps_w1", tag="tr")
                    for i in range(2):
                        words_t(ps[:, i], w1raw[:, 2 * half + i, :])
                    if half == 0:
                        nc.vector.tensor_copy(out=gw1w[:, 0:2], in_=ps[:].rearrange("q t u m -> q t m u"))
                    else:
                        nc.scalar.copy(out=gw1w[:, 2:4], in_=ps[:].rearrange("q t u m -> q t m u"))
                nc.vector.quantize_mx(out=w1c[:].bitcast(FP8X4), scales=w1s[:], in_=gw1[:])

                gw2 = pre.tile([P, 4 * NOUT], BF16, name="gw2", align_bytes=64)
                ps = ps_tr.tile([P, 2, 2, P], F32, name="ps_w2", tag="tr")
                words_t(ps[:, 0], w2raw[:])
                nc.vector.tensor_copy(out=gw2[:].bitcast(F32).rearrange("q (n u) -> q n u", u=2), in_=ps[:, 0].rearrange("q u n -> q n u"))
                nc.vector.quantize_mx(out=w2c[:].bitcast(FP8X4), scales=w2s[:], in_=gw2[:])

            mx = actx.enter_context(tc.tile_pool(name="mx", bufs=2))
            one = actx.enter_context(tc.tile_pool(name="one", bufs=1))

            g1, c1, s1, g2, c2, s2, ps2, xs, xc, y0 = {}, {}, {}, {}, {}, {}, {}, {}, {}, {}

            def turn(c):
                g1[c] = mx.tile([P, 4 * HID], BF16, name="g1", tag="g1", align_bytes=64)
                g1w = g1[c][:].bitcast(F32).rearrange("q (t b u) -> q t b u", t=TPC, u=2)
                for half in range(2):
                    ps = ps_tr.tile([P, 2, 2, P], F32, name="ps_h1", tag="tr")
                    for i in range(2):
                        words_t(ps[:, i], h1c[c][:, 2 * half + i, :])
                    if c == 0 and half == 0:
                        nc.vector.tensor_copy(out=g1w[:, 0:2], in_=ps[:].rearrange("q t u b -> q t b u"))
                    else:
                        nc.scalar.copy(out=g1w[:, 2 * half : 2 * half + 2], in_=ps[:].rearrange("q t u b -> q t b u"))

            def quant1(c):
                c1[c] = mx.tile([P, HID], U32, name="c1", tag="c1", align_bytes=64)
                s1[c] = mx.tile([P, HID], U8, name="s1", tag="s1", align_bytes=64)
                nc.vector.quantize_mx(out=c1[c][:].bitcast(FP8X4), scales=s1[c][:], in_=g1[c][:])

            def stage1(c):
                hc = mx.tile([P, 4, HID], BF16, name="hc", tag="hc")
                for t in range(4):
                    bank = ps_s1.tile([P, HID], BANK_DT, name="bank", tag="s1")
                    nc.tensor.matmul_mx(
                        out=bank[:],
                        lhsT=w1c[:, t * P : (t + 1) * P].bitcast(FP8X4),
                        lhsT_scale=w1s[:, t * P : (t + 1) * P],
                        rhs=c1[c][:].bitcast(FP8X4),
                        rhs_scale=s1[c][:],
                        start=True,
                        stop=True,
                    )
                    if c == 0 and t >= 2:
                        nc.vector.tensor_scalar(out=hc[:, t, :], in0=bank[:], scalar1=b1f[:, t : t + 1], scalar2=0.0, op0=ALU.add, op1=ALU.max)
                    else:
                        nc.scalar.activation(out=hc[:, t, :], in_=bank[:], func=ACT.Relu, bias=b1f[:, t : t + 1], scale=1.0)
                g2[c] = mx.tile([P, 4 * HID], BF16, name="g2", tag="g2", align_bytes=64)
                if c in V_INTERLEAVES:
                    nc.vector.tensor_copy(out=g2[c][:].rearrange("q (b t) -> q b t", t=4), in_=hc[:].rearrange("q t b -> q b t"))
                else:
                    nc.scalar.copy(out=g2[c][:].rearrange("q (b t) -> q b t", t=4), in_=hc[:].rearrange("q t b -> q b t"))

            bnr = {}

            def bias_rows(c):
                bnr[c] = mx.tile([P, TPC, NOUT], F32, name="bnr", tag="bnr")
                for i in range(TPC):
                    nc.scalar.activation(out=bnr[c][:, i, :], in_=bof[:], func=ACT.Copy, scale=nrf[:, c * TPC + i : c * TPC + i + 1])

            def quant2(c):
                c2[c] = mx.tile([P, HID], U32, name="c2", tag="c2", align_bytes=64)
                s2[c] = mx.tile([P, HID], U8, name="s2", tag="s2", align_bytes=64)
                nc.vector.quantize_mx(out=c2[c][:].bitcast(FP8X4), scales=s2[c][:], in_=g2[c][:])
                ps2[c] = ps_s2.tile([P, TPC, NOUT], F32, name="ps2", tag="s2")
                for i in range(TPC):
                    nc.tensor.matmul_mx(
                        out=ps2[c][:, i, :],
                        lhsT=c2[c][:, i * P : (i + 1) * P].bitcast(FP8X4),
                        lhsT_scale=s2[c][:, i * P : (i + 1) * P],
                        rhs=w2c[:].bitcast(FP8X4),
                        rhs_scale=w2s[:],
                        start=True,
                        stop=True,
                    )

            def make_x(c):
                lo, hi = c * TPC, (c + 1) * TPC
                xs[c] = mx.tile([P, TPC, NOUT], F32, name="xs", tag="xs")
                xc[c] = mx.tile([P, TPC, NOUT], F32, name="xc", tag="xc")
                for i in range(TPC):
                    stt(xs[c][:, i, :], ps2[c][:, i, :], nrf[:, lo + i : lo + i + 1], bnr[c][:, i, :])
                nc.vector.tensor_scalar(out=xc[c][:], in0=xs[c][:], scalar1=-2.0, scalar2=2.0, op0=ALU.max, op1=ALU.min)
                nc.sync.dma_start(out=x_out[:, lo:hi, :], in_=xs[c][:])
                nc.sync.dma_start(out=xc_out[:, lo:hi, :], in_=xc[c][:])

            def lay_a(c):
                if c >= NVCH:
                    psx = ps_tt.tile([P, TPC, P], F32, name="psx", tag="tt")
                    for i in range(TPC):
                        nc.tensor.transpose(psx[:, i, :], xs[c][:, i, :], ident_f[:])
                    nc.scalar.copy(out=xT[:, (c - NVCH) * TPC : (c - NVCH + 1) * TPC, :], in_=psx[:])
                y0[c] = mx.tile([P, nsg(c), NOUT, TPC], F32, name="y0", tag="y0")
                nc.scalar.copy(out=y0[c][:, 0], in_=xc[c][:].rearrange("p t n -> p n t"))
                if c < NVCH:
                    nc.scalar.copy(out=y0[c][:, 1], in_=xs[c][:].rearrange("p t n -> p n t"))

            def lay_b(c):
                lo = c * TPC
                for i in range(TPC):
                    sq = mx.tile([P, NOUT], F32, name="sq", tag="sq")
                    nc.scalar.activation(out=sq[:], in_=xs[c][:, i, :], func=ACT.Square, accum_out=r0[:, lo + i : lo + i + 1])
                    sq = mx.tile([P, NOUT], F32, name="sq", tag="sq")
                    nc.scalar.activation(out=sq[:], in_=xc[c][:, i, :], func=ACT.Square, accum_out=r0[:, NT + lo + i : NT + lo + i + 1])

            half = NOUT // 2
            th0 = levels[0][0] / 2

            def early_im(c):
                g0, g1 = sg0(c), sg0(c) + nsg(c)
                b0 = y0[c][:, :, half:NOUT, :]
                nc.scalar.activation(out=za[:, g0:g1, 1, 0:half, :], in_=b0, func=ACT.Copy, scale=math.sin(th0))
                nc.scalar.activation(out=za[:, g0:g1, 1, half:NOUT, :], in_=b0, func=ACT.Copy, scale=-math.sin(th0))

            def early_01(c):
                g0, g1 = sg0(c), sg0(c) + nsg(c)
                a0, b0 = y0[c][:, :, 0:half, :], y0[c][:, :, half:NOUT, :]
                stt(za[:, g0:g1, 0, 0:half, :], b0, math.cos(th0), a0)
                stt(za[:, g0:g1, 0, half:NOUT, :], b0, -math.cos(th0), a0)
                stage(1, za, zb, g0, g1)

            def early_2(c):
                stage(2, zb, za, sg0(c), sg0(c) + nsg(c))

            def early_3(c):
                if NEARLY > 3:
                    stage(3, za, zb, sg0(c), sg0(c) + nsg(c))

            def live(c):
                return 0 <= c < NCH

            def tables():
                kf = one.tile([P, 1], F32, name="kf")
                nc.vector.tensor_copy(out=kf[:], in_=ki[:])
                mrow = one.tile([P, NOUT], F32, name="mrow")
                nc.vector.memset(mrow[:, 0:1], -1.0)
                for n in range(NSTAGE):
                    w = 1 << n
                    nc.vector.tensor_scalar(out=mrow[:, w : 2 * w], in0=mrow[:, 0:w], scalar1=float(4 << (NSTAGE - 1 - n)), scalar2=None, op0=ALU.add)
                aa = one.tile([P, 2 * NOUT], F32, name="aa")
                nc.vector.tensor_scalar(out=aa[:, 0:NOUT], in0=mrow[:], scalar1=kf[:, 0:1], scalar2=None, op0=ALU.mult)
                nc.vector.tensor_scalar(out=aa[:, NOUT : 2 * NOUT], in0=mrow[:], scalar1=kf[:, 0:1], scalar2=-128.0, op0=ALU.mult, op1=ALU.add)
                ai = one.tile([P, 2 * NOUT], I32, name="ai")
                nc.vector.tensor_copy(out=ai[:], in_=aa[:])
                am = one.tile([P, 2 * NOUT], I32, name="am")
                nc.vector.tensor_scalar(out=am[:], in0=ai[:], scalar1=511, scalar2=None, op0=ALU.bitwise_and)
                xf = one.tile([P, 2 * NOUT], F32, name="xf")
                nc.vector.tensor_scalar(out=xf[:], in0=am[:], scalar1=-256.0, scalar2=None, op0=ALU.add)
                xa = one.tile([P, 2 * NOUT], F32, name="xa")
                nc.scalar.activation(out=xa[:], in_=xf[:], func=ACT.Abs)
                nc.scalar.activation(out=cs[:], in_=xa[:], func=ACT.Sin, scale=math.pi / 256, bias=-math.pi / 2)


            for r in range(NCH + 2):
                if 3 <= r + 2 < NCH:
                    load(r + 2)
                if live(r - 2):
                    make_x(r - 2)
                if live(r - 2):
                    lay_a(r - 2)
                    early_im(r - 2)
                if live(r - 3):
                    early_3(r - 3)
                if live(r):
                    turn(r)
                if live(r - 2):
                    early_01(r - 2)
                if live(r - 1):
                    stage1(r - 1)
                if live(r):
                    quant1(r)
                if live(r - 1):
                    bias_rows(r - 1)
                    quant2(r - 1)
                if r == 1:
                    tables()
                if live(r - 2):
                    early_2(r - 2)
                    lay_b(r - 2)
            early_3(NCH - 1)

        with ExitStack() as bctx:
            late = bctx.enter_context(tc.tile_pool(name="late", bufs=1))
            two = bctx.enter_context(tc.tile_pool(name="two", bufs=2))
            ps_fin = bctx.enter_context(tc.psum_pool(name="ps_fin", bufs=1))
            ps_tp = bctx.enter_context(tc.psum_pool(name="ps_tp", bufs=2))
            ps_th = bctx.enter_context(tc.psum_pool(name="ps_th", bufs=2))
            ps_of = bctx.enter_context(tc.psum_pool(name="ps_of", bufs=2))
            noff = NT - TPC * NVCH
            th2 = late.tile([P, NCH, NOUT, TPC], F32, name="th2")
            thoff = late.tile([P, noff, NOUT], F32, name="thoff")
            for c in range(NCH):
                lo, hi = c * TPC, (c + 1) * TPC
                pst = ps_tp.tile([P, TPC, P], BF16, name="pst", tag="tp")
                for i in range(TPC):
                    nc.tensor.transpose(pst[:, i, :], tpad[:, lo + i, :], ident_b[:])
                tT = two.tile([P, TPC, P], F32, name="tT", tag="tT")
                nc.scalar.copy(out=tT[:], in_=pst[:])
                pth = ps_th.tile([P, TPC, NOUT], F32, name="pth", tag="th")
                for i in range(TPC):
                    nc.tensor.matmul(out=pth[:, i, :], lhsT=tT[:, i, :], rhs=cs[:, 0:NOUT], start=True, stop=True)
                nc.scalar.activation(out=th2[:, c], in_=pth[:].rearrange("p t f -> p f t"), func=ACT.Copy, scale=-2.0)
                if c >= NVCH:
                    nc.scalar.activation(out=thoff[:, lo - TPC * NVCH : hi - TPC * NVCH, :], in_=pth[:], func=ACT.Copy, scale=-2.0)
            sqo = late.tile([P, noff, 2 * NOUT], F32, name="sqo")
            for j in range(noff // 2):
                pof = ps_of.tile([P, 2, 2 * NOUT], F32, name="pof", tag="of")
                for i in range(2):
                    nc.tensor.matmul(out=pof[:, i, :], lhsT=xT[:, 2 * j + i, :], rhs=cs[:], start=True, stop=True)
                nc.scalar.activation(out=sqo[:, 2 * j : 2 * j + 2, :], in_=pof[:], func=ACT.Square)
            q0 = late.tile([P, 2], F32, name="q0")
            r0sq = late.tile([P, 2 * NT], F32, name="r0sq")
            for y in range(2):
                nc.scalar.activation(out=r0sq[:, y * NT : (y + 1) * NT], in_=r0[:, y * NT : (y + 1) * NT], func=ACT.Square, accum_out=q0[:, y : y + 1])

            pair = [za, zb]
            for s in range(NEARLY, NSTAGE - 1):
                stage(s, pair[(s + 1) % 2], pair[s % 2], 0, NSG)
            poff = late.tile([P, noff, NOUT], F32, name="poff")
            nc.vector.tensor_tensor(out=poff[:], in0=sqo[:, :, 0:NOUT], in1=sqo[:, :, NOUT : 2 * NOUT], op=ALU.add)
            nc.vector.tensor_tensor(out=thoff[:], in0=thoff[:], in1=poff[:], op=ALU.add)
            nc.scalar.activation(out=poff[:], in_=thoff[:], func=ACT.Square, accum_out=acc[:, 0, 7:8])
            q0h = late.tile([P, 2], F32, name="q0h")
            nc.vector.tensor_scalar(out=q0h[:], in0=q0[:], scalar1=0.5, scalar2=None, op0=ALU.mult)

            npn = (NOUT // 2) // NPIECE
            for k in range(NPIECE):
                plus(NSTAGE - 1, zb, za, 0, NSG, list(range(k * npn, (k + 1) * npn)))
                rows = slice(2 * k * npn, 2 * (k + 1) * npn, 2)
                spare = slice(2 * k * npn + 1, 2 * (k + 1) * npn, 2)
                nc.scalar.activation(out=both(zb, 0, NSG)[:, :, spare, :], in_=both(za, 0, NSG)[:, :, rows, :], func=ACT.Square)
            cuts = [(0, 4), (4, 8), (8, NSG)]
            upper, bottom = slice(0, NOUT, 2), slice(1, NOUT, 2)
            for g0, g1 in cuts:
                minus(NSTAGE - 1, zb, za, g0, g1)
                nc.scalar.activation(out=both(zb, g0, g1)[:, :, upper, :], in_=both(za, g0, g1)[:, :, bottom, :], func=ACT.Square)

            cols = [0, 0]

            def finish(freqs, rows, g0, g1):
                nc.vector.tensor_tensor(out=zb[:, g0:g1, 0, rows, :], in0=zb[:, g0:g1, 0, rows, :], in1=zb[:, g0:g1, 1, rows, :], op=ALU.add)
                e1 = min(g1, 2 * NVCH)
                parts = []
                if g0 < e1:
                    parts.append((slice(g0, e1, 2), slice(g0 // 2, e1 // 2), 1))
                    parts.append((slice(g0 + 1, e1, 2), slice(g0 // 2, e1 // 2), 0))
                if g1 > 2 * NVCH:
                    t0 = max(g0, 2 * NVCH)
                    parts.append((slice(t0, g1), slice(t0 - NVCH, g1 - NVCH), 1))
                for gs, ch, y in parts:
                    nc.vector.tensor_tensor(out=zb[:, gs, 1, rows, :], in0=zb[:, gs, 0, rows, :], in1=th2[:, ch, freqs, :], op=ALU.add)
                for gs, ch, y in parts:
                    nc.scalar.activation(out=za[:, gs, 0, rows, :], in_=zb[:, gs, 1, rows, :], func=ACT.Square, accum_out=acc[:, y, cols[y] : cols[y] + 1])
                    cols[y] += 1

            finish(upper, bottom, 0, NSG)
            for g0, g1 in cuts:
                finish(bottom, upper, g0, g1)

            sd = late.tile([P, 2], F32, name="sd")
            nc.vector.tensor_reduce(out=sd[:], in_=acc[:], axis=AX.X, op=ALU.add)
            stt(wide[:, 0:2], sd[:], 1.0 / 256.0, q0h[:], ALU.subtract)
            pfin = ps_fin.tile([P, P], F32, name="pfin")
            nc.tensor.transpose(pfin[:], wide[:], ident_f[:])
            junk = late.tile([P, P], F32, name="junk")
            res = late.tile([P, 1], F32, name="res")
            nc.scalar.activation(out=junk[:], in_=pfin[:], func=ACT.Copy, scale=1.0 / (ROWS * NLAG), accum_out=res[:])
            nc.sync.dma_start(out=out_1.rearrange("(a b) -> a b", a=1), in_=res[0:1, 0:1])
            nc.sync.dma_start(out=out_3.rearrange("(a b) -> a b", a=1), in_=res[1:2, 0:1])
